import numpy as np
import ml_dtypes


def mxq(x, axis, fmt="e4m3"):
    dtype, down = {"e4m3": (ml_dtypes.float8_e4m3fn, 7), "e5m2": (ml_dtypes.float8_e5m2, 14)}[fmt]
    v = np.moveaxis(np.asarray(x, np.float32).astype(ml_dtypes.bfloat16).astype(np.float64), axis, -1)
    blocks = v.reshape(v.shape[:-1] + (-1, 32))
    amax = np.abs(blocks).max(-1, keepdims=True)
    byte = np.maximum(np.where(amax > 0, np.frexp(amax)[1] - 1 + 127, 0) - down, 1)
    scale = np.exp2(byte - 127.0)
    codes = (blocks / scale).astype(np.float32).astype(dtype).astype(np.float64)
    return np.moveaxis((codes * scale).reshape(v.shape), -1, axis)


WIDE = False


def mx_kscale(k):
    if not WIDE:
        return np.ones(k)
    levels = np.array([10, -10, 5, -5, 0])
    if k % 512:
        return np.exp2(np.random.permutation(np.resize(levels, k // 32))).repeat(32)
    a = np.empty((k // 512, 16))
    for p in range(k // 512):
        a[p, :8] = np.random.permutation(np.resize(levels, 8))
        for g in range(8):
            far = levels[np.abs(levels - a[p, g]) >= 10]
            a[p, g + 8] = far[np.random.randint(len(far))]
    return np.exp2(a.ravel()).repeat(32)


BF16 = ml_dtypes.bfloat16


def bf(x):
    return np.asarray(x, np.float32).astype(BF16)


def f64(x):
    return np.asarray(x).astype(np.float64)


B, T, D, H, HK, HD, W = 2, 1024, 1024, 8, 2, 128, 512
HALF = HD // 2
ROPE_BASE = 10000.0
EPS = 1e-6


def rope_cos_sin():
    inv_freq = 1.0 / ROPE_BASE ** (np.arange(0, HD, 2) / HD)
    freqs = np.arange(T)[:, None] * inv_freq[None, :]
    emb = np.concatenate([freqs, freqs], axis=-1)
    return np.cos(emb), np.sin(emb)


def rotate_half(u):
    return np.concatenate([-u[..., HALF:], u[..., :HALF]], axis=-1)


def heads(u, n):
    return u.reshape(B, T, n, HD).transpose(0, 2, 1, 3)


def l2_gain(u, gamma):
    return u / (np.sqrt((u * u).sum(-1, keepdims=True)) + EPS) * gamma


def draw0():
    s = mx_kscale(D)
    return {"x": bf(np.random.standard_normal((B, T, D)) * s),
            "wq": bf(np.random.standard_normal((H * HD, D)) / np.sqrt(D) / s[None, :]),
            "wk": bf(np.random.standard_normal((HK * HD, D)) / np.sqrt(D) / s[None, :]),
            "wv": bf(np.random.standard_normal((HK * HD, D)) * 2.0 / np.sqrt(D) / s[None, :]),
            "gamma_q": bf(np.sqrt(HD) * (1.0 + 0.1 * np.random.standard_normal(HD))),
            "gamma_k": bf(np.sqrt(HD) * (1.0 + 0.1 * np.random.standard_normal(HD)))}


def core(x, wq, wk, wv, gamma_q, gamma_k):
    xq = mxq(f64(x), 2, "e4m3")
    q = heads(xq @ mxq(f64(wq), 1, "e4m3").T, H)
    k = heads(xq @ mxq(f64(wk), 1, "e4m3").T, HK)
    v = heads(xq @ mxq(f64(wv), 1, "e4m3").T, HK)
    cos, sin = rope_cos_sin()
    q = q * cos + rotate_half(q) * sin
    k = k * cos + rotate_half(k) * sin
    q = l2_gain(q, f64(gamma_q))
    k = l2_gain(k, f64(gamma_k))
    return q, k, v


def e4m3fn_bytes(y):
    return np.clip(np.asarray(y, np.float64), -448.0, 448.0).astype(np.float32).astype(ml_dtypes.float8_e4m3fn).view(np.uint8)


def e4m3fn_values(b):
    return np.asarray(b, np.uint8).view(ml_dtypes.float8_e4m3fn).astype(np.float64)


def setup_inputs():
    d = draw0()
    x0 = np.asarray(d['x']).astype(np.float64)
    s = (np.max(np.abs(x0), axis=(0, 1), keepdims=True) / 448.0).astype(np.float32)
    out = {}
    for k, v in d.items():
        if k == 'x':
            out['x_bytes'] = e4m3fn_bytes(x0 / s.astype(np.float64))
            out['x_scale'] = s
        else:
            out[k] = v
    return out


def reference(x_bytes, x_scale, wq, wk, wv, gamma_q, gamma_k):
    return core(e4m3fn_values(x_bytes) * x_scale.astype(np.float64), wq, wk, wv, gamma_q, gamma_k)

@@ -1,0 +1,328 @@
+from contextlib import ExitStack
+
+import concourse.mybir as mybir
+from concourse.masks import make_identity
+
+F32 = mybir.dt.float32
+BF16 = mybir.dt.bfloat16
+U32 = mybir.dt.uint32
+U8 = mybir.dt.uint8
+I32 = mybir.dt.int32
+FP8 = mybir.dt.float8_e4m3fn
+FP8X4 = mybir.dt.float8_e4m3fn_x4
+ALU = mybir.AluOpType
+ACT = mybir.ActivationFunctionType
+
+P = 128
+D = 1024
+HD = 128
+HALF = 64
+ROPE_BASE = 10000.0
+EPS = 1e-6
+GROUPS = 8
+BANKS = 3
+UNITS = 48
+LEAD = 4
+LAG = 3
+TWO_PI = 6.283185307179586
+
+FLOPS = 2 * 2048 * 1024 * 1536
+
+
+def tile_gqaattention_pa_kernel(tc, x_bytes, x_scale, wq, wk, wv, gamma_q, gamma_k, out_0, out_1, out_2):
+    nc = tc.nc
+    with ExitStack() as ctx:
+        keep = ctx.enter_context(tc.tile_pool(name="keep", bufs=1))
+        rings = ctx.enter_context(tc.tile_pool(name="rings", bufs=1))
+        banks = ctx.enter_context(tc.psum_pool(name="banks", bufs=1))
+        taken = {}
+
+        def ring(pool, base, depth, shape, dtype, align=None):
+            k = taken.get(base, 0)
+            taken[base] = k + 1
+            slot = "%s%d" % (base, k % depth)
+            if align is None:
+                return pool.tile(shape, dtype, name=slot)
+            return pool.tile(shape, dtype, name=slot, align_bytes=align)
+
+        one = keep.tile([P, 1], F32, name="one")
+        nc.vector.memset(one[:], 1.0)
+        first = keep.tile([P, 1], F32, name="first")
+        nc.scalar.activation(out=first[:], in_=one[:], func=ACT.Sin)
+
+        xb = keep.tile([P, GROUPS, 2 * D], U8, name="x_bytes_sb")
+        x_rows = x_bytes.rearrange("b t k -> (b t) k").rearrange("(g p i) k -> p g (i k)", p=P, i=2)
+        scale_t = keep.tile([P, 2, 4], F32, name="scale_t")
+        wraw = keep.tile([P, 12, D], BF16, name="wraw")
+        gam = keep.tile([P, 2, HD], BF16, name="gam")
+        wq_rows = wq.rearrange("(a p) k -> p a k", p=P)
+
+        nc.sync.dma_start(out=xb[:, 0:1, :], in_=x_rows[:, 0:1, :])
+        with nc.allow_non_contiguous_dma(reason="four scales to a partition and pass"):
+            nc.sync.dma_start(out=scale_t[:], in_=x_scale.rearrange("a b (c p t) -> p (a b c) t", p=P, t=4))
+        nc.sync.dma_start(out=gam[:, 0, :], in_=gamma_q.partition_broadcast(P))
+        nc.sync.dma_start(out=gam[:, 1, :], in_=gamma_k.partition_broadcast(P))
+        nc.sync.dma_start(out=wraw[:, 0:2, :], in_=wq_rows[:, 0:2, :])
+        nc.sync.dma_start(out=wraw[:, 2:4, :], in_=wq_rows[:, 2:4, :])
+        nc.sync.dma_start(out=xb[:, 1:2, :], in_=x_rows[:, 1:2, :])
+        nc.sync.dma_start(out=wraw[:, 4:8, :], in_=wq_rows[:, 4:8, :])
+        nc.sync.dma_start(out=wraw[:, 8:10, :], in_=wk.rearrange("(a p) k -> p a k", p=P))
+        nc.sync.dma_start(out=wraw[:, 10:12, :], in_=wv.rearrange("(a p) k -> p a k", p=P))
+        nc.sync.dma_start(out=xb[:, 2:4, :], in_=x_rows[:, 2:4, :])
+        nc.sync.dma_start(out=xb[:, 4:8, :], in_=x_rows[:, 4:8, :])
+
+        tpos = keep.tile([P, 8], F32, name="tpos")
+        nc.gpsimd.iota(tpos[:], pattern=[[256, 4], [1, 2]], base=0, channel_multiplier=2,
+                       allow_small_or_imprecise_dtypes=True)
+        ident = keep.tile([P, P], F32, name="ident")
+        make_identity(nc, ident[:])
+
+
+        turns = keep.tile([P, 8], F32, name="turns")
+        nc.vector.tensor_scalar(out=turns[:], in0=tpos[:], scalar1=1.0 / TWO_PI, scalar2=None, op0=ALU.mult)
+        freq = keep.tile([P, HALF], F32, name="freq")
+        nc.vector.memset(freq[:, 0:1], 1.0)
+        for m in (1, 2, 4, 8, 16, 32):
+            nc.vector.tensor_scalar(out=freq[:, m:2 * m], in0=freq[:, 0:m], scalar1=ROPE_BASE ** (-m / HALF),
+                                    scalar2=None, op0=ALU.mult)
+        phi = keep.tile([P, 8, HALF], F32, name="phi")
+        nc.vector.tensor_tensor(out=phi[:], in0=turns[:].unsqueeze(2).to_broadcast([P, 8, HALF]),
+                                in1=freq[:].unsqueeze(1).to_broadcast([P, 8, HALF]), op=ALU.mult)
+        whole_i = keep.tile([P, 8 * HALF], I32, name="whole_i")
+        phi_f = phi[:].rearrange("p a j -> p (a j)")
+        nc.vector.tensor_copy(out=whole_i[:], in_=phi_f)
+        whole = keep.tile([P, 8 * HALF], F32, name="whole")
+        nc.vector.tensor_copy(out=whole[:], in_=whole_i[:])
+        frac = keep.tile([P, 8 * HALF], F32, name="frac")
+        nc.vector.tensor_tensor(out=frac[:], in0=phi_f, in1=whole[:], op=ALU.subtract)
+        negs = keep.tile([P, 8, HALF], F32, name="negs")
+        negs_f = negs[:].rearrange("p a j -> p (a j)")
+        nc.vector.scalar_tensor_tensor(out=negs_f, in0=frac[:], scalar=0.5, in1=frac[:], op0=ALU.is_gt,
+                                       op1=ALU.subtract)
+        cq = keep.tile([P, 8 * HALF], F32, name="cq")
+        nc.vector.tensor_scalar(out=cq[:], in0=negs_f, scalar1=-1.0, scalar2=0.25, op0=ALU.mult, op1=ALU.add)
+        negc = keep.tile([P, 8, HALF], F32, name="negc")
+        nc.vector.scalar_tensor_tensor(out=negc[:].rearrange("p a j -> p (a j)"), in0=cq[:], scalar=0.5, in1=cq[:],
+                                       op0=ALU.is_gt, op1=ALU.subtract)
+        cos_t = keep.tile([P, 8, HALF], F32, name="cos_t")
+        sin2 = keep.tile([P, 8, 2, HALF], F32, name="sin2")
+        rope = keep.tile([P, 2, 2, 8, HD], F32, name="rope")
+
+        def sines():
+            nc.scalar.activation(out=cos_t[:], in_=negc[:], func=ACT.Sin, scale=-TWO_PI)
+            nc.scalar.activation(out=sin2[:, :, 0, :], in_=negs[:], func=ACT.Sin, scale=TWO_PI)
+            nc.scalar.activation(out=sin2[:, :, 1, :], in_=negs[:], func=ACT.Sin, scale=-TWO_PI)
+
+        def gains(a):
+            gis = slice(2 * a, 2 * a + 2)
+            for w in range(2):
+                gv = gam[:, w, :].rearrange("p (s j) -> p s j", s=2).unsqueeze(1).to_broadcast([P, 2, 2, HALF])
+                nc.gpsimd.tensor_tensor(
+                    out=rope[:, w, 0, gis, :].rearrange("p a (s j) -> p a s j", s=2),
+                    in0=cos_t[:, gis, :].unsqueeze(2).to_broadcast([P, 2, 2, HALF]), in1=gv, op=ALU.mult)
+                nc.gpsimd.tensor_tensor(
+                    out=rope[:, w, 1, gis, :].rearrange("p a (s j) -> p a s j", s=2),
+                    in0=sin2[:, gis, :, :], in1=gv, op=ALU.mult)
+
+        wc = keep.tile([P, 2, 1536], U32, name="wc", align_bytes=64)
+        wsc = keep.tile([P, 2, 1536], U8, name="wsc", align_bytes=64)
+
+        def turn_words(words, dst):
+            t = ring(banks, "tp", 2, [P, 2, 2, P], F32)
+            for c in range(2):
+                for u in range(2):
+                    nc.tensor.transpose(t[:, c, u, :], words[:, 256 * c + u:256 * (c + 1):2], ident[:])
+            nc.scalar.copy(out=dst, in_=t[:].rearrange("p c u r -> p c r u"))
+
+        def wturn(b):
+            wg = ring(rings, "wg", 2, [P, 2, 512, 2], F32, 64)
+            for al in range(4):
+                turn_words(wraw[:, 4 * b + al, :].bitcast(F32), wg[:, :, P * al:P * (al + 1), :])
+            return wg
+
+        def wquant(b, wg):
+            for c in range(2):
+                cols = slice(512 * b, 512 * (b + 1))
+                nc.vector.quantize_mx(out=wc[:, c, cols].bitcast(FP8X4), scales=wsc[:, c, cols],
+                                      in_=wg[:, c].rearrange("p f u -> p (f u)").bitcast(BF16))
+
+        def widen(g):
+            xs = ring(rings, "xs", 2, [P, 2, D], BF16)
+            for i in range(2):
+                nc.scalar.copy(out=xs[:, i, :], in_=xb[:, g, D * i:D * (i + 1)].bitcast(FP8))
+            return xs
+
+        def turn(xs):
+            xg = ring(rings, "xg", 2, [P, 2, 2, P, 4], BF16, 64)
+            for i in range(2):
+                words = xs[:, i, :].bitcast(F32)
+                t = ring(banks, "tp", 2, [P, 2, 2, P], F32)
+                for c in range(2):
+                    for u in range(2):
+                        nc.tensor.transpose(t[:, c, u, :], words[:, 256 * c + u:256 * (c + 1):2], ident[:])
+                for c in range(2):
+                    nc.vector.tensor_tensor(
+                        out=xg[:, i, c].rearrange("p r (u e) -> p r u e", u=2),
+                        in0=scale_t[:, c, :].rearrange("p (u e) -> p u e", u=2).unsqueeze(1).to_broadcast([P, P, 2, 2]),
+                        in1=t[:, c].rearrange("p u r -> p (u r)").bitcast(BF16).rearrange("p (u r e) -> p r u e", u=2, e=2),
+                        op=ALU.mult)
+            return xg
+
+        def quant(xg):
+            xc = ring(rings, "xc", 4, [P, 512], U32, 64)
+            xsc = ring(rings, "xsc", 4, [P, 512], U8, 64)
+            nc.vector.quantize_mx(out=xc[:].bitcast(FP8X4), scales=xsc[:],
+                                  in_=xg[:].rearrange("p i c r t -> p (i c r t)"))
+            return xc, xsc
+
+        q_dst = [out_0[bt].rearrange("h (a p i) d -> a p h (i d)", a=4, p=P, i=2) for bt in range(2)]
+        k_dst = [out_1[bt].rearrange("h (a p i) d -> a p h (i d)", a=4, p=P, i=2) for bt in range(2)]
+        v_dst = [out_2[bt].rearrange("h (a p i) d -> a p h (i d)", a=4, p=P, i=2) for bt in range(2)]
+
+        xs_of = {}
+        xg_of = {}
+        xq = {}
+        un = {}
+        pr = {}
+        ot = {}
+
+        def where(m):
+            g, r = divmod(m, 6)
+            b, i = divmod(r, 2)
+            return g, b, i, (4 if b < 2 else 2)
+
+        def mx(m):
+            g, b, i, nh = where(m)
+            xc, xsc = xq[g]
+            acc = ring(banks, "acc", 6, [P, 512], F32)
+            for c in range(2):
+                lc = slice(256 * i + P * c, 256 * i + P * (c + 1))
+                rc = slice(512 * b, 512 * (b + 1))
+                nc.tensor.matmul_mx(out=acc[:], lhsT=xc[:, lc].bitcast(FP8X4), lhsT_scale=xsc[:, lc],
+                                    rhs=wc[:, c, rc].bitcast(FP8X4), rhs_scale=wsc[:, c, rc],
+                                    start=(c == 0), stop=(c == 1))
+            un[m] = {"acc": acc}
+
+        def rope_mul(m):
+            g, b, i, nh = where(m)
+            gi = 2 * (g % 4) + i
+            acc = un[m]["acc"]
+            t1 = ring(rings, "ta", 4, [P, 4, HD], F32)
+            t2 = ring(rings, "tb", 4, [P, 4, HD], F32)
+            swapped = acc[:, 0:nh * HD].rearrange("p (h s j) -> p h s j", s=2, j=HALF)[:, :, ::-1, :]
+            if b < 2:
+                nc.vector.tensor_tensor(out=t1[:], in0=rope[:, 0, 0, gi, :].unsqueeze(1).to_broadcast([P, nh, HD]),
+                                        in1=acc[:].rearrange("p (h d) -> p h d", d=HD), op=ALU.mult)
+                nc.vector.tensor_tensor(
+                    out=t2[:].rearrange("p h (s j) -> p h s j", s=2),
+                    in0=rope[:, 0, 1, gi, :].rearrange("p (s j) -> p s j", s=2).unsqueeze(1).to_broadcast(
+                        [P, nh, 2, HALF]),
+                    in1=swapped, op=ALU.mult)
+            else:
+                rinv = pr[(g, 1)]["rinv"]
+                for h in range(nh):
+                    col = rinv[:, i * nh + h:i * nh + h + 1]
+                    nc.vector.scalar_tensor_tensor(out=t1[:, h, :], in0=acc[:, HD * h:HD * (h + 1)], scalar=col,
+                                                   in1=rope[:, 1, 0, gi, :], op0=ALU.mult, op1=ALU.mult)
+                    nc.vector.scalar_tensor_tensor(out=t2[:, h, :].rearrange("p (s j) -> p s j", s=2),
+                                                   in0=swapped[:, h], scalar=col,
+                                                   in1=rope[:, 1, 1, gi, :].rearrange("p (s j) -> p s j", s=2),
+                                                   op0=ALU.mult, op1=ALU.mult)
+            un[m]["t1"] = t1
+            un[m]["t2"] = t2
+
+        def rope_add(m):
+            g, b, i, nh = where(m)
+            if b < 2:
+                rot = ring(rings, "rot", 6, [P, nh, HD], F32)
+                un[m]["rot"] = rot
+                dst = rot[:]
+            else:
+                dst = ot[(g, b)][:, 0:2, i, :]
+            nc.gpsimd.tensor_tensor(out=dst, in0=un[m]["t1"][:, 0:nh], in1=un[m]["t2"][:, 0:nh], op=ALU.add)
+
+        def norms(m):
+            g, b, i, nh = where(m)
+            kind = 0 if b < 2 else 1
+            if i == 0:
+                o = ring(rings, "o", 6, [P, 4, 2, HD], F32)
+                ot[(g, b)] = o
+            if i == 0 and b != 1:
+                ss = ring(rings, "ss", 4, [P, 16], F32)
+                pr[(g, kind)] = {"ss": ss}
+            ss = pr[(g, kind)]["ss"]
+            acc = un[m]["acc"]
+            base = (b % 2) * 8 + i * nh
+            for h in range(nh):
+                junk = ring(rings, "junk", 4, [P, HD], BF16)
+                nc.scalar.activation(out=junk[:], in_=acc[:, HD * h:HD * (h + 1)], func=ACT.Square,
+                                     accum_out=ss[:, base + h:base + h + 1])
+            if b == 2:
+                nc.scalar.copy(out=ot[(g, b)][:, 2:4, i, :], in_=acc[:, 256:512].rearrange("p (h d) -> p h d", d=HD))
+            if i == 1 and b != 0:
+                n = 16 if b == 1 else 4
+                nrm = ring(rings, "nrm", 4, [P, 16], F32)
+                nc.scalar.activation(out=nrm[:, 0:n], in_=ss[:, 0:n], func=ACT.Sqrt)
+                nrm_e = ring(rings, "nrme", 4, [P, 16], F32)
+                nc.scalar.activation(out=nrm_e[:, 0:n], in_=nrm[:, 0:n], func=ACT.Copy, bias=EPS)
+                rinv = ring(rings, "rinv", 4, [P, 16], F32)
+                nc.vector.reciprocal(out=rinv[:, 0:n], in_=nrm_e[:, 0:n])
+                pr[(g, kind)]["rinv"] = rinv
+
+        def finish(m):
+            g, b, i, nh = where(m)
+            o = ot[(g, b)]
+            if b < 2:
+                rinv = pr[(g, 0)]["rinv"]
+                rot = un[m]["rot"]
+                base = b * 8 + i * nh
+                for h in range(nh):
+                    nc.scalar.activation(out=o[:, h, i, :], in_=rot[:, h, :], func=ACT.Copy,
+                                         scale=rinv[:, base + h:base + h + 1])
+            if i == 1:
+                bt, a = divmod(g, 4)
+                ov = o[:].rearrange("p h i d -> p h (i d)")
+                if b < 2:
+                    nc.sync.dma_start(out=q_dst[bt][a][:, 4 * b:4 * (b + 1), :], in_=ov)
+                else:
+                    nc.sync.dma_start(out=k_dst[bt][a], in_=ov[:, 0:2, :])
+                    nc.sync.dma_start(out=v_dst[bt][a], in_=ov[:, 2:4, :])
+
+        def feed(m):
+            mx(m)
+            norms(m)
+
+        xs_of[0] = widen(0)
+        sines()
+        xg_of[0] = turn(xs_of[0])
+        wg0 = wturn(0)
+        gains(0)
+        xq[0] = quant(xg_of[0])
+        wquant(0, wg0)
+        feed(0)
+        feed(1)
+        wquant(1, wturn(1))
+        feed(2)
+        feed(3)
+        xs_of[1] = widen(1)
+        xg_of[1] = turn(xs_of[1])
+        gains(1)
+        gains(2)
+        gains(3)
+
+        for m in range(UNITS + LAG):
+            if m == 0:
+                wquant(2, wturn(2))
+            for g in range(1, GROUPS):
+                if m == 6 * g - 9:
+                    xs_of[g] = widen(g)
+                    xg_of[g] = turn(xs_of[g])
+                if m == max(6 * g - 6, 0):
+                    xq[g] = quant(xg_of[g])
+            if m + LEAD < UNITS:
+                feed(m + LEAD)
+            if m < UNITS:
+                rope_mul(m)
+                rope_add(m)
+            if m >= LAG:
+                finish(m - LAG)

@@ -54,14 +54,18 @@ def tile_gqaattention_pa_kernel(tc, x_bytes, x_scale, wq, wk, wv, gamma_q, gamma
         x_rows = x_bytes.rearrange("b t k -> (b t) k").rearrange("(g p i) k -> p g (i k)", p=P, i=2)
         scale_t = keep.tile([P, 2, 4], F32, name="scale_t")
         wraw = keep.tile([P, 12, D], BF16, name="wraw")
-        gam = keep.tile([P, 2, HD], BF16, name="gam")
+        gam_rows = keep.tile([P, 2 * HD], BF16, name="gam_rows")
+        nc.vector.memset(gam_rows[:], 0.0)
+        ones_sq = keep.tile([P, P], BF16, name="ones_sq")
+        nc.vector.memset(ones_sq[:], 1.0)
+        gam = keep.tile([P, 2, HD], F32, name="gam")
         wq_rows = wq.rearrange("(a p) k -> p a k", p=P)
 
         nc.sync.dma_start(out=xb[:, 0:1, :], in_=x_rows[:, 0:1, :])
         with nc.allow_non_contiguous_dma(reason="four scales to a partition and pass"):
             nc.sync.dma_start(out=scale_t[:], in_=x_scale.rearrange("a b (c p t) -> p (a b c) t", p=P, t=4))
-        nc.sync.dma_start(out=gam[:, 0, :], in_=gamma_q.partition_broadcast(P))
-        nc.sync.dma_start(out=gam[:, 1, :], in_=gamma_k.partition_broadcast(P))
+        nc.sync.dma_start(out=gam_rows[0:1, 0:HD], in_=gamma_q.unsqueeze(0))
+        nc.sync.dma_start(out=gam_rows[0:1, HD:2 * HD], in_=gamma_k.unsqueeze(0))
         nc.sync.dma_start(out=wraw[:, 0:2, :], in_=wq_rows[:, 0:2, :])
         nc.sync.dma_start(out=wraw[:, 2:4, :], in_=wq_rows[:, 2:4, :])
         nc.sync.dma_start(out=xb[:, 1:2, :], in_=x_rows[:, 1:2, :])
@@ -76,6 +80,10 @@ def tile_gqaattention_pa_kernel(tc, x_bytes, x_scale, wq, wk, wv, gamma_q, gamma
                        allow_small_or_imprecise_dtypes=True)
         ident = keep.tile([P, P], F32, name="ident")
         make_identity(nc, ident[:])
+
+        gam_ps = ring(banks, "tp", 2, [P, 2, 2, P], F32)
+        nc.tensor.matmul(out=gam_ps[:, 0].rearrange("p u r -> p (u r)"), lhsT=ones_sq[:], rhs=gam_rows[:], start=True, stop=True)
+        nc.scalar.copy(out=gam[:].rearrange("p w d -> p (w d)"), in_=gam_ps[:, 0].rearrange("p u r -> p (u r)"))
 
 
         turns = keep.tile([P, 8], F32, name="turns")

@@ -161,13 +161,20 @@ def tile_gqaattention_pa_kernel(tc, x_bytes, x_scale, wq, wk, wv, gamma_q, gamma
             return xs
 
         def turn(xs):
-            xg = ring(rings, "xg", 2, [P, 2, 2, P, 4], BF16, 64)
+            ts = []
             for i in range(2):
                 words = xs[:, i, :].bitcast(F32)
                 t = ring(banks, "tp", 2, [P, 2, 2, P], F32)
                 for c in range(2):
                     for u in range(2):
                         nc.tensor.transpose(t[:, c, u, :], words[:, 256 * c + u:256 * (c + 1):2], ident[:])
+                ts.append(t)
+            return ts
+
+        def scaled(ts):
+            xg = ring(rings, "xg", 2, [P, 2, 2, P, 4], BF16, 64)
+            for i in range(2):
+                t = ts[i]
                 for c in range(2):
                     nc.vector.tensor_tensor(
                         out=xg[:, i, c].rearrange("p r (u e) -> p r u e", u=2),
@@ -189,6 +196,7 @@ def tile_gqaattention_pa_kernel(tc, x_bytes, x_scale, wq, wk, wv, gamma_q, gamma
 
         xs_of = {}
         xg_of = {}
+        tp_of = {}
         xq = {}
         un = {}
         pr = {}
@@ -267,15 +275,24 @@ def tile_gqaattention_pa_kernel(tc, x_bytes, x_scale, wq, wk, wv, gamma_q, gamma
                                      accum_out=ss[:, base + h:base + h + 1])
             if b == 2:
                 nc.scalar.copy(out=ot[(g, b)][:, 2:4, i, :], in_=acc[:, 256:512].rearrange("p (h d) -> p h d", d=HD))
-            if i == 1 and b != 0:
-                n = 16 if b == 1 else 4
-                nrm = ring(rings, "nrm", 4, [P, 16], F32)
-                nc.scalar.activation(out=nrm[:, 0:n], in_=ss[:, 0:n], func=ACT.Sqrt)
-                nrm_e = ring(rings, "nrme", 4, [P, 16], F32)
-                nc.scalar.activation(out=nrm_e[:, 0:n], in_=nrm[:, 0:n], func=ACT.Copy, bias=EPS)
-                rinv = ring(rings, "rinv", 4, [P, 16], F32)
-                nc.vector.reciprocal(out=rinv[:, 0:n], in_=nrm_e[:, 0:n])
-                pr[(g, kind)]["rinv"] = rinv
+
+        def root(g, kind):
+            n = 4 if kind else 16
+            nrm = ring(rings, "nrm", 4, [P, 16], F32)
+            nc.scalar.activation(out=nrm[:, 0:n], in_=pr[(g, kind)]["ss"][:, 0:n], func=ACT.Sqrt)
+            pr[(g, kind)]["nrm"] = nrm
+
+        def plus_eps(g, kind):
+            n = 4 if kind else 16
+            nrm_e = ring(rings, "nrme", 4, [P, 16], F32)
+            nc.scalar.activation(out=nrm_e[:, 0:n], in_=pr[(g, kind)]["nrm"][:, 0:n], func=ACT.Copy, bias=EPS)
+            pr[(g, kind)]["nrm_e"] = nrm_e
+
+        def invert(g, kind):
+            n = 4 if kind else 16
+            rinv = ring(rings, "rinv", 4, [P, 16], F32)
+            nc.vector.reciprocal(out=rinv[:, 0:n], in_=pr[(g, kind)]["nrm_e"][:, 0:n])
+            pr[(g, kind)]["rinv"] = rinv
 
         def finish(m):
             g, b, i, nh = where(m)
@@ -302,7 +319,7 @@ def tile_gqaattention_pa_kernel(tc, x_bytes, x_scale, wq, wk, wv, gamma_q, gamma
 
         xs_of[0] = widen(0)
         sines()
-        xg_of[0] = turn(xs_of[0])
+        xg_of[0] = scaled(turn(xs_of[0]))
         wg0 = wturn(0)
         gains(0)
         xq[0] = quant(xg_of[0])
@@ -312,8 +329,9 @@ def tile_gqaattention_pa_kernel(tc, x_bytes, x_scale, wq, wk, wv, gamma_q, gamma
         wquant(1, wturn(1))
         feed(2)
         feed(3)
+        root(0, 0)
         xs_of[1] = widen(1)
-        xg_of[1] = turn(xs_of[1])
+        xg_of[1] = scaled(turn(xs_of[1]))
         gains(1)
         gains(2)
         gains(3)
@@ -321,16 +339,30 @@ def tile_gqaattention_pa_kernel(tc, x_bytes, x_scale, wq, wk, wv, gamma_q, gamma
         for m in range(UNITS + LAG):
             if m == 0:
                 wquant(2, wturn(2))
+            gm, r = divmod(m, 6)
             for g in range(1, GROUPS):
+                if g > 1 and m == max(6 * g - 12, 1):
+                    tp_of[g] = turn(widen(g))
                 if m == 6 * g - 9:
-                    xs_of[g] = widen(g)
-                    xg_of[g] = turn(xs_of[g])
+                    xg_of[g] = scaled(tp_of[g])
                 if m == max(6 * g - 6, 0):
                     xq[g] = quant(xg_of[g])
+            if gm < GROUPS and r == 1:
+                invert(gm, 0)
+            if gm < GROUPS and r == 3:
+                invert(gm, 1)
             if m + LEAD < UNITS:
                 feed(m + LEAD)
+            if gm < GROUPS and r == 0:
+                plus_eps(gm, 0)
+            if gm < GROUPS and r == 2:
+                plus_eps(gm, 1)
             if m < UNITS:
                 rope_mul(m)
                 rope_add(m)
             if m >= LAG:
                 finish(m - LAG)
+            if gm + 1 < GROUPS and r == 5:
+                root(gm + 1, 0)
+            if gm < GROUPS and r == 1:
+                root(gm, 1)

from contextlib import ExitStack

import concourse.mybir as mybir
from concourse.masks import make_identity

F32 = mybir.dt.float32
BF16 = mybir.dt.bfloat16
U32 = mybir.dt.uint32
U8 = mybir.dt.uint8
I32 = mybir.dt.int32
FP8 = mybir.dt.float8_e4m3fn
FP8X4 = mybir.dt.float8_e4m3fn_x4
ALU = mybir.AluOpType
ACT = mybir.ActivationFunctionType

P = 128
D = 1024
HD = 128
HALF = 64
ROPE_BASE = 10000.0
EPS = 1e-6
GROUPS = 8
BANKS = 3
UNITS = 48
LEAD = 4
LAG = 3
TWO_PI = 6.283185307179586

FLOPS = 2 * 2048 * 1024 * 1536


def tile_gqaattention_pa_kernel(tc, x_bytes, x_scale, wq, wk, wv, gamma_q, gamma_k, out_0, out_1, out_2):
    nc = tc.nc
    with ExitStack() as ctx:
        keep = ctx.enter_context(tc.tile_pool(name="keep", bufs=1))
        rings = ctx.enter_context(tc.tile_pool(name="rings", bufs=1))
        banks = ctx.enter_context(tc.psum_pool(name="banks", bufs=1))
        taken = {}

        def ring(pool, base, depth, shape, dtype, align=None):
            k = taken.get(base, 0)
            taken[base] = k + 1
            slot = "%s%d" % (base, k % depth)
            if align is None:
                return pool.tile(shape, dtype, name=slot)
            return pool.tile(shape, dtype, name=slot, align_bytes=align)

        one = keep.tile([P, 1], F32, name="one")
        nc.vector.memset(one[:], 1.0)
        first = keep.tile([P, 1], F32, name="first")
        nc.scalar.activation(out=first[:], in_=one[:], func=ACT.Sin)

        xb = keep.tile([P, GROUPS, 2 * D], U8, name="x_bytes_sb")
        x_rows = x_bytes.rearrange("b t k -> (b t) k").rearrange("(g p i) k -> p g (i k)", p=P, i=2)
        scale_t = keep.tile([P, 2, 4], F32, name="scale_t")
        wraw = keep.tile([P, 12, D], BF16, name="wraw")
        gam_rows = keep.tile([P, 2 * HD], BF16, name="gam_rows")
        nc.vector.memset(gam_rows[:], 0.0)
        ones_sq = keep.tile([P, P], BF16, name="ones_sq")
        nc.vector.memset(ones_sq[:], 1.0)
        gam = keep.tile([P, 2, HD], F32, name="gam")
        wq_rows = wq.rearrange("(a p) k -> p a k", p=P)

        nc.sync.dma_start(out=xb[:, 0:1, :], in_=x_rows[:, 0:1, :])
        with nc.allow_non_contiguous_dma(reason="four scales to a partition and pass"):
            nc.sync.dma_start(out=scale_t[:], in_=x_scale.rearrange("a b (c p t) -> p (a b c) t", p=P, t=4))
        nc.sync.dma_start(out=gam_rows[0:1, 0:HD], in_=gamma_q.unsqueeze(0))
        nc.sync.dma_start(out=gam_rows[0:1, HD:2 * HD], in_=gamma_k.unsqueeze(0))
        nc.sync.dma_start(out=wraw[:, 0:2, :], in_=wq_rows[:, 0:2, :])
        nc.sync.dma_start(out=wraw[:, 2:4, :], in_=wq_rows[:, 2:4, :])
        nc.sync.dma_start(out=xb[:, 1:2, :], in_=x_rows[:, 1:2, :])
        nc.sync.dma_start(out=wraw[:, 4:8, :], in_=wq_rows[:, 4:8, :])
        nc.sync.dma_start(out=wraw[:, 8:10, :], in_=wk.rearrange("(a p) k -> p a k", p=P))
        nc.sync.dma_start(out=wraw[:, 10:12, :], in_=wv.rearrange("(a p) k -> p a k", p=P))
        nc.sync.dma_start(out=xb[:, 2:4, :], in_=x_rows[:, 2:4, :])
        nc.sync.dma_start(out=xb[:, 4:8, :], in_=x_rows[:, 4:8, :])

        tpos = keep.tile([P, 8], F32, name="tpos")
        nc.gpsimd.iota(tpos[:], pattern=[[256, 4], [1, 2]], base=0, channel_multiplier=2,
                       allow_small_or_imprecise_dtypes=True)
        ident = keep.tile([P, P], F32, name="ident")
        make_identity(nc, ident[:])

        gam_ps = ring(banks, "tp", 2, [P, 2, 2, P], F32)
        nc.tensor.matmul(out=gam_ps[:, 0].rearrange("p u r -> p (u r)"), lhsT=ones_sq[:], rhs=gam_rows[:], start=True, stop=True)
        nc.scalar.copy(out=gam[:].rearrange("p w d -> p (w d)"), in_=gam_ps[:, 0].rearrange("p u r -> p (u r)"))


        turns = keep.tile([P, 8], F32, name="turns")
        nc.vector.tensor_scalar(out=turns[:], in0=tpos[:], scalar1=1.0 / TWO_PI, scalar2=None, op0=ALU.mult)
        freq = keep.tile([P, HALF], F32, name="freq")
        nc.vector.memset(freq[:, 0:1], 1.0)
        for m in (1, 2, 4, 8, 16, 32):
            nc.vector.tensor_scalar(out=freq[:, m:2 * m], in0=freq[:, 0:m], scalar1=ROPE_BASE ** (-m / HALF),
                                    scalar2=None, op0=ALU.mult)
        phi = keep.tile([P, 8, HALF], F32, name="phi")
        nc.vector.tensor_tensor(out=phi[:], in0=turns[:].unsqueeze(2).to_broadcast([P, 8, HALF]),
                                in1=freq[:].unsqueeze(1).to_broadcast([P, 8, HALF]), op=ALU.mult)
        whole_i = keep.tile([P, 8 * HALF], I32, name="whole_i")
        phi_f = phi[:].rearrange("p a j -> p (a j)")
        nc.vector.tensor_copy(out=whole_i[:], in_=phi_f)
        whole = keep.tile([P, 8 * HALF], F32, name="whole")
        nc.vector.tensor_copy(out=whole[:], in_=whole_i[:])
        frac = keep.tile([P, 8 * HALF], F32, name="frac")
        nc.vector.tensor_tensor(out=frac[:], in0=phi_f, in1=whole[:], op=ALU.subtract)
        negs = keep.tile([P, 8, HALF], F32, name="negs")
        negs_f = negs[:].rearrange("p a j -> p (a j)")
        nc.vector.scalar_tensor_tensor(out=negs_f, in0=frac[:], scalar=0.5, in1=frac[:], op0=ALU.is_gt,
                                       op1=ALU.subtract)
        cq = keep.tile([P, 8 * HALF], F32, name="cq")
        nc.vector.tensor_scalar(out=cq[:], in0=negs_f, scalar1=-1.0, scalar2=0.25, op0=ALU.mult, op1=ALU.add)
        negc = keep.tile([P, 8, HALF], F32, name="negc")
        nc.vector.scalar_tensor_tensor(out=negc[:].rearrange("p a j -> p (a j)"), in0=cq[:], scalar=0.5, in1=cq[:],
                                       op0=ALU.is_gt, op1=ALU.subtract)
        cos_t = keep.tile([P, 8, HALF], F32, name="cos_t")
        sin2 = keep.tile([P, 8, 2, HALF], F32, name="sin2")
        rope = keep.tile([P, 2, 2, 8, HD], F32, name="rope")

        def sines():
            nc.scalar.activation(out=cos_t[:], in_=negc[:], func=ACT.Sin, scale=-TWO_PI)
            nc.scalar.activation(out=sin2[:, :, 0, :], in_=negs[:], func=ACT.Sin, scale=TWO_PI)
            nc.scalar.activation(out=sin2[:, :, 1, :], in_=negs[:], func=ACT.Sin, scale=-TWO_PI)

        def gains(a):
            gis = slice(2 * a, 2 * a + 2)
            for w in range(2):
                gv = gam[:, w, :].rearrange("p (s j) -> p s j", s=2).unsqueeze(1).to_broadcast([P, 2, 2, HALF])
                nc.gpsimd.tensor_tensor(
                    out=rope[:, w, 0, gis, :].rearrange("p a (s j) -> p a s j", s=2),
                    in0=cos_t[:, gis, :].unsqueeze(2).to_broadcast([P, 2, 2, HALF]), in1=gv, op=ALU.mult)
                nc.gpsimd.tensor_tensor(
                    out=rope[:, w, 1, gis, :].rearrange("p a (s j) -> p a s j", s=2),
                    in0=sin2[:, gis, :, :], in1=gv, op=ALU.mult)

        wc = keep.tile([P, 2, 1536], U32, name="wc", align_bytes=64)
        wsc = keep.tile([P, 2, 1536], U8, name="wsc", align_bytes=64)

        def turn_words(words, dst):
            t = ring(banks, "tp", 2, [P, 2, 2, P], F32)
            for c in range(2):
                for u in range(2):
                    nc.tensor.transpose(t[:, c, u, :], words[:, 256 * c + u:256 * (c + 1):2], ident[:])
            nc.scalar.copy(out=dst, in_=t[:].rearrange("p c u r -> p c r u"))

        def wturn(b):
            wg = ring(rings, "wg", 2, [P, 2, 512, 2], F32, 64)
            for al in range(4):
                turn_words(wraw[:, 4 * b + al, :].bitcast(F32), wg[:, :, P * al:P * (al + 1), :])
            return wg

        def wquant(b, wg):
            for c in range(2):
                cols = slice(512 * b, 512 * (b + 1))
                nc.vector.quantize_mx(out=wc[:, c, cols].bitcast(FP8X4), scales=wsc[:, c, cols],
                                      in_=wg[:, c].rearrange("p f u -> p (f u)").bitcast(BF16))

        def widen(g):
            xs = ring(rings, "xs", 2, [P, 2, D], BF16)
            for i in range(2):
                nc.scalar.copy(out=xs[:, i, :], in_=xb[:, g, D * i:D * (i + 1)].bitcast(FP8))
            return xs

        def turn(xs):
            ts = []
            for i in range(2):
                words = xs[:, i, :].bitcast(F32)
                t = ring(banks, "tp", 2, [P, 2, 2, P], F32)
                for c in range(2):
                    for u in range(2):
                        nc.tensor.transpose(t[:, c, u, :], words[:, 256 * c + u:256 * (c + 1):2], ident[:])
                ts.append(t)
            return ts

        def scaled(ts):
            xg = ring(rings, "xg", 2, [P, 2, 2, P, 4], BF16, 64)
            for i in range(2):
                t = ts[i]
                for c in range(2):
                    nc.vector.tensor_tensor(
                        out=xg[:, i, c].rearrange("p r (u e) -> p r u e", u=2),
                        in0=scale_t[:, c, :].rearrange("p (u e) -> p u e", u=2).unsqueeze(1).to_broadcast([P, P, 2, 2]),
                        in1=t[:, c].rearrange("p u r -> p (u r)").bitcast(BF16).rearrange("p (u r e) -> p r u e", u=2, e=2),
                        op=ALU.mult)
            return xg

        def quant(xg):
            xc = ring(rings, "xc", 4, [P, 512], U32, 64)
            xsc = ring(rings, "xsc", 4, [P, 512], U8, 64)
            nc.vector.quantize_mx(out=xc[:].bitcast(FP8X4), scales=xsc[:],
                                  in_=xg[:].rearrange("p i c r t -> p (i c r t)"))
            return xc, xsc

        q_dst = [out_0[bt].rearrange("h (a p i) d -> a p h (i d)", a=4, p=P, i=2) for bt in range(2)]
        k_dst = [out_1[bt].rearrange("h (a p i) d -> a p h (i d)", a=4, p=P, i=2) for bt in range(2)]
        v_dst = [out_2[bt].rearrange("h (a p i) d -> a p h (i d)", a=4, p=P, i=2) for bt in range(2)]

        xs_of = {}
        xg_of = {}
        tp_of = {}
        xq = {}
        un = {}
        pr = {}
        ot = {}

        def where(m):
            g, r = divmod(m, 6)
            b, i = divmod(r, 2)
            return g, b, i, (4 if b < 2 else 2)

        def mx(m):
            g, b, i, nh = where(m)
            xc, xsc = xq[g]
            acc = ring(banks, "acc", 6, [P, 512], F32)
            for c in range(2):
                lc = slice(256 * i + P * c, 256 * i + P * (c + 1))
                rc = slice(512 * b, 512 * (b + 1))
                nc.tensor.matmul_mx(out=acc[:], lhsT=xc[:, lc].bitcast(FP8X4), lhsT_scale=xsc[:, lc],
                                    rhs=wc[:, c, rc].bitcast(FP8X4), rhs_scale=wsc[:, c, rc],
                                    start=(c == 0), stop=(c == 1))
            un[m] = {"acc": acc}

        def rope_mul(m):
            g, b, i, nh = where(m)
            gi = 2 * (g % 4) + i
            acc = un[m]["acc"]
            t1 = ring(rings, "ta", 4, [P, 4, HD], F32)
            t2 = ring(rings, "tb", 4, [P, 4, HD], F32)
            swapped = acc[:, 0:nh * HD].rearrange("p (h s j) -> p h s j", s=2, j=HALF)[:, :, ::-1, :]
            if b < 2:
                nc.vector.tensor_tensor(out=t1[:], in0=rope[:, 0, 0, gi, :].unsqueeze(1).to_broadcast([P, nh, HD]),
                                        in1=acc[:].rearrange("p (h d) -> p h d", d=HD), op=ALU.mult)
                nc.vector.tensor_tensor(
                    out=t2[:].rearrange("p h (s j) -> p h s j", s=2),
                    in0=rope[:, 0, 1, gi, :].rearrange("p (s j) -> p s j", s=2).unsqueeze(1).to_broadcast(
                        [P, nh, 2, HALF]),
                    in1=swapped, op=ALU.mult)
            else:
                rinv = pr[(g, 1)]["rinv"]
                for h in range(nh):
                    col = rinv[:, i * nh + h:i * nh + h + 1]
                    nc.vector.scalar_tensor_tensor(out=t1[:, h, :], in0=acc[:, HD * h:HD * (h + 1)], scalar=col,
                                                   in1=rope[:, 1, 0, gi, :], op0=ALU.mult, op1=ALU.mult)
                    nc.vector.scalar_tensor_tensor(out=t2[:, h, :].rearrange("p (s j) -> p s j", s=2),
                                                   in0=swapped[:, h], scalar=col,
                                                   in1=rope[:, 1, 1, gi, :].rearrange("p (s j) -> p s j", s=2),
                                                   op0=ALU.mult, op1=ALU.mult)
            un[m]["t1"] = t1
            un[m]["t2"] = t2

        def rope_add(m):
            g, b, i, nh = where(m)
            if b < 2:
                rot = ring(rings, "rot", 6, [P, nh, HD], F32)
                un[m]["rot"] = rot
                dst = rot[:]
            else:
                dst = ot[(g, b)][:, 0:2, i, :]
            nc.gpsimd.tensor_tensor(out=dst, in0=un[m]["t1"][:, 0:nh], in1=un[m]["t2"][:, 0:nh], op=ALU.add)

        def norms(m):
            g, b, i, nh = where(m)
            kind = 0 if b < 2 else 1
            if i == 0:
                o = ring(rings, "o", 6, [P, 4, 2, HD], F32)
                ot[(g, b)] = o
            if i == 0 and b != 1:
                ss = ring(rings, "ss", 4, [P, 16], F32)
                pr[(g, kind)] = {"ss": ss}
            ss = pr[(g, kind)]["ss"]
            acc = un[m]["acc"]
            base = (b % 2) * 8 + i * nh
            for h in range(nh):
                junk = ring(rings, "junk", 4, [P, HD], BF16)
                nc.scalar.activation(out=junk[:], in_=acc[:, HD * h:HD * (h + 1)], func=ACT.Square,
                                     accum_out=ss[:, base + h:base + h + 1])
            if b == 2:
                nc.scalar.copy(out=ot[(g, b)][:, 2:4, i, :], in_=acc[:, 256:512].rearrange("p (h d) -> p h d", d=HD))

        def root(g, kind):
            n = 4 if kind else 16
            nrm = ring(rings, "nrm", 4, [P, 16], F32)
            nc.scalar.activation(out=nrm[:, 0:n], in_=pr[(g, kind)]["ss"][:, 0:n], func=ACT.Sqrt)
            pr[(g, kind)]["nrm"] = nrm

        def plus_eps(g, kind):
            n = 4 if kind else 16
            nrm_e = ring(rings, "nrme", 4, [P, 16], F32)
            nc.scalar.activation(out=nrm_e[:, 0:n], in_=pr[(g, kind)]["nrm"][:, 0:n], func=ACT.Copy, bias=EPS)
            pr[(g, kind)]["nrm_e"] = nrm_e

        def invert(g, kind):
            n = 4 if kind else 16
            rinv = ring(rings, "rinv", 4, [P, 16], F32)
            nc.vector.reciprocal(out=rinv[:, 0:n], in_=pr[(g, kind)]["nrm_e"][:, 0:n])
            pr[(g, kind)]["rinv"] = rinv

        def finish(m):
            g, b, i, nh = where(m)
            o = ot[(g, b)]
            if b < 2:
                rinv = pr[(g, 0)]["rinv"]
                rot = un[m]["rot"]
                base = b * 8 + i * nh
                for h in range(nh):
                    nc.scalar.activation(out=o[:, h, i, :], in_=rot[:, h, :], func=ACT.Copy,
                                         scale=rinv[:, base + h:base + h + 1])
            if i == 1:
                bt, a = divmod(g, 4)
                ov = o[:].rearrange("p h i d -> p h (i d)")
                if b < 2:
                    nc.sync.dma_start(out=q_dst[bt][a][:, 4 * b:4 * (b + 1), :], in_=ov)
                else:
                    nc.sync.dma_start(out=k_dst[bt][a], in_=ov[:, 0:2, :])
                    nc.sync.dma_start(out=v_dst[bt][a], in_=ov[:, 2:4, :])

        def feed(m):
            mx(m)
            norms(m)

        xs_of[0] = widen(0)
        sines()
        xg_of[0] = scaled(turn(xs_of[0]))
        wg0 = wturn(0)
        gains(0)
        xq[0] = quant(xg_of[0])
        wquant(0, wg0)
        feed(0)
        feed(1)
        wquant(1, wturn(1))
        feed(2)
        feed(3)
        root(0, 0)
        xs_of[1] = widen(1)
        xg_of[1] = scaled(turn(xs_of[1]))
        gains(1)
        gains(2)
        gains(3)

        for m in range(UNITS + LAG):
            if m == 0:
                wquant(2, wturn(2))
            gm, r = divmod(m, 6)
            for g in range(1, GROUPS):
                if g > 1 and m == max(6 * g - 12, 1):
                    tp_of[g] = turn(widen(g))
                if m == 6 * g - 9:
                    xg_of[g] = scaled(tp_of[g])
                if m == max(6 * g - 6, 0):
                    xq[g] = quant(xg_of[g])
            if gm < GROUPS and r == 1:
                invert(gm, 0)
            if gm < GROUPS and r == 3:
                invert(gm, 1)
            if m + LEAD < UNITS:
                feed(m + LEAD)
            if gm < GROUPS and r == 0:
                plus_eps(gm, 0)
            if gm < GROUPS and r == 2:
                plus_eps(gm, 1)
            if m < UNITS:
                rope_mul(m)
                rope_add(m)
            if m >= LAG:
                finish(m - LAG)
            if gm + 1 < GROUPS and r == 5:
                root(gm + 1, 0)
            if gm < GROUPS and r == 1:
                root(gm, 1)
